import numpy as np
import ml_dtypes

BF16 = ml_dtypes.bfloat16


def bf(x):
    return np.asarray(x, np.float32).astype(BF16)


def f32(x):
    return np.asarray(x, np.float32)


def f64(x):
    return np.asarray(x).astype(np.float64)


def striped(idx):
    return np.tile(idx.reshape(-1, 16).T, (8, 1))


S, D, M, N = 4096, 128, 512, 2048
EPS = 1e-12


def setup_inputs():
    return {"table": bf(np.random.standard_normal((S, D))), "w": bf(np.random.standard_normal((D, M))), "b": f32(0.1 * np.random.standard_normal((M, 1))), "offs": striped(np.random.permutation(np.tile(np.arange(S), 2))[:N])}


def reference(table, w, b, offs):
    idx = offs[:16].T.reshape(-1)
    t = f64(table)
    tn = t / np.maximum(np.sqrt(np.sum(t * t, axis=1, keepdims=True)), EPS)
    return f64(w).T @ tn[idx].T + f64(b)

@@ -1,0 +1,92 @@
+import concourse.mybir as mybir
+from concourse.masks import make_identity
+
+P = 128
+S, D, M, N = 4096, 128, 512, 2048
+EPS = 1e-12
+
+BLOCKS = S // P
+CHUNK = 8
+CHUNKS = BLOCKS // CHUNK
+PIECE = 512
+PIECES = N // PIECE
+MB = M // P
+
+FLOPS = 2 * D * M * N
+
+BF16, F32, U16 = mybir.dt.bfloat16, mybir.dt.float32, mybir.dt.uint16
+ACT = mybir.ActivationFunctionType
+ADD = mybir.AluOpType.add
+
+
+def tile_rulee_kernel(tc, table, w, b, offs, out):
+    nc = tc.nc
+    with (
+        tc.tile_pool(name="held", bufs=1) as held,
+        tc.tile_pool(name="rows", bufs=CHUNKS) as rows,
+        tc.tile_pool(name="work", bufs=2) as work,
+        tc.tile_pool(name="staged", bufs=6) as staged,
+        tc.psum_pool(name="flip", bufs=2) as flip,
+        tc.psum_pool(name="bias_flip", bufs=1) as bias_flip,
+        tc.psum_pool(name="products", bufs=4) as products,
+    ):
+        table_blocks = table.rearrange("(t p) d -> p t d", p=P)
+        x_chunks = []
+        for c in range(CHUNKS):
+            x = rows.tile([P, CHUNK, D], BF16, name="x")
+            nc.sync.dma_start(x[:], table_blocks[:, c * CHUNK : (c + 1) * CHUNK, :])
+            x_chunks.append(x)
+        offsets = held.tile([P, N // 16], U16, name="offsets")
+        nc.sync.dma_start(offsets[:], offs)
+        w_sb = held.tile([D, M], BF16, name="w_sb")
+        nc.scalar.dma_start(w_sb[:], w)
+
+        ident_f32 = held.tile([P, P], F32, name="ident_f32")
+        make_identity(nc, ident_f32[:])
+        ident = held.tile([P, P], BF16, name="ident")
+        make_identity(nc, ident[:])
+        b_rows = held.tile([P, P], F32, name="b_rows")
+        nc.vector.memset(b_rows[:], 0.0)
+        nc.scalar.dma_start(b_rows[0:MB, :], b.rearrange("(mb p) one -> mb (p one)", p=P))
+        b_cols = bias_flip.tile([P, P], F32, name="b_cols")
+        nc.tensor.transpose(b_cols[:], b_rows[:], ident_f32[:])
+        bias = held.tile([P, MB], F32, name="bias")
+        nc.vector.tensor_copy(bias[:], b_cols[:, 0:MB])
+
+        tnT = held.tile([D, S], BF16, name="tnT")
+        for c in range(CHUNKS):
+            x = x_chunks[c]
+            squares = work.tile([P, CHUNK, D], F32, name="squares")
+            nc.scalar.activation(squares[:], x[:], ACT.Square)
+            sumsq = work.tile([P, CHUNK], F32, name="sumsq")
+            nc.vector.tensor_reduce(sumsq[:], squares[:], axis=mybir.AxisListType.X, op=ADD)
+            nc.vector.tensor_scalar_max(sumsq[:], sumsq[:], EPS * EPS)
+            norm = work.tile([P, CHUNK], F32, name="norm")
+            nc.scalar.activation(norm[:], sumsq[:], ACT.Sqrt)
+            inv_norm = work.tile([P, CHUNK], F32, name="inv_norm")
+            nc.vector.reciprocal(inv_norm[:], norm[:])
+            tn = work.tile([P, CHUNK, D], BF16, name="tn")
+            for t in range(CHUNK):
+                nc.vector.tensor_scalar_mul(tn[:, t, :], x[:, t, :], inv_norm[:, t : t + 1])
+            flipped = flip.tile([D, CHUNK * P], BF16, name="flipped")
+            for t in range(CHUNK):
+                nc.tensor.transpose(flipped[:, t * P : (t + 1) * P], tn[:, t, :], ident[:])
+            nc.scalar.copy(tnT[:, c * CHUNK * P : (c + 1) * CHUNK * P], flipped[:])
+
+        k = PIECE // 16
+        for j in range(PIECES):
+            for mb in range(MB):
+                product = products.tile([P, PIECE], F32, name="product")
+                nc.tensor.matmul(
+                    product[:],
+                    w_sb[:, mb * P : (mb + 1) * P],
+                    tnT[:].indirect(offsets[:, j * k : (j + 1) * k]),
+                    start=True,
+                    stop=True,
+                )
+                result = staged.tile([P, PIECE], F32, name="result")
+                if mb % 2 == 0:
+                    nc.vector.tensor_scalar_add(result[:], product[:], bias[:, mb : mb + 1])
+                else:
+                    nc.scalar.activation(result[:], product[:], ACT.Identity, bias=bias[:, mb : mb + 1])
+                nc.sync.dma_start(out[mb * P : (mb + 1) * P, j * PIECE : (j + 1) * PIECE], result[:])

@@ -5,9 +5,8 @@ P = 128
 S, D, M, N = 4096, 128, 512, 2048
 EPS = 1e-12
 
-BLOCKS = S // P
-CHUNK = 8
-CHUNKS = BLOCKS // CHUNK
+CHUNK = 4
+CHUNKS = S // (CHUNK * P)
 PIECE = 512
 PIECES = N // PIECE
 MB = M // P
@@ -16,7 +15,6 @@ FLOPS = 2 * D * M * N
 
 BF16, F32, U16 = mybir.dt.bfloat16, mybir.dt.float32, mybir.dt.uint16
 ACT = mybir.ActivationFunctionType
-ADD = mybir.AluOpType.add
 
 
 def tile_rulee_kernel(tc, table, w, b, offs, out):
@@ -24,9 +22,9 @@ def tile_rulee_kernel(tc, table, w, b, offs, out):
     with (
         tc.tile_pool(name="held", bufs=1) as held,
         tc.tile_pool(name="rows", bufs=CHUNKS) as rows,
-        tc.tile_pool(name="work", bufs=2) as work,
+        tc.tile_pool(name="work", bufs=3) as work,
         tc.tile_pool(name="staged", bufs=6) as staged,
-        tc.psum_pool(name="flip", bufs=2) as flip,
+        tc.psum_pool(name="flip", bufs=3) as flip,
         tc.psum_pool(name="bias_flip", bufs=1) as bias_flip,
         tc.psum_pool(name="products", bufs=4) as products,
     ):
@@ -41,6 +39,10 @@ def tile_rulee_kernel(tc, table, w, b, offs, out):
         w_sb = held.tile([D, M], BF16, name="w_sb")
         nc.scalar.dma_start(w_sb[:], w)
 
+        one = held.tile([P, 1], F32, name="one")
+        nc.vector.memset(one[:], 1.0)
+        nc.scalar.activation(one[:], one[:], ACT.Sqrt)
+
         ident_f32 = held.tile([P, P], F32, name="ident_f32")
         make_identity(nc, ident_f32[:])
         ident = held.tile([P, P], BF16, name="ident")
@@ -54,12 +56,17 @@ def tile_rulee_kernel(tc, table, w, b, offs, out):
         nc.vector.tensor_copy(bias[:], b_cols[:, 0:MB])
 
         tnT = held.tile([D, S], BF16, name="tnT")
-        for c in range(CHUNKS):
-            x = x_chunks[c]
-            squares = work.tile([P, CHUNK, D], F32, name="squares")
-            nc.scalar.activation(squares[:], x[:], ACT.Square)
+        sumsq_chunks, tn_chunks = {}, {}
+
+        def sum_squares(c):
             sumsq = work.tile([P, CHUNK], F32, name="sumsq")
-            nc.vector.tensor_reduce(sumsq[:], squares[:], axis=mybir.AxisListType.X, op=ADD)
+            for t in range(CHUNK):
+                squares = work.tile([P, D], BF16, name="squares")
+                nc.scalar.activation(squares[:], x_chunks[c][:, t, :], ACT.Square, accum_out=sumsq[:, t : t + 1])
+            sumsq_chunks[c] = sumsq
+
+        def scale(c):
+            sumsq = sumsq_chunks[c]
             nc.vector.tensor_scalar_max(sumsq[:], sumsq[:], EPS * EPS)
             norm = work.tile([P, CHUNK], F32, name="norm")
             nc.scalar.activation(norm[:], sumsq[:], ACT.Sqrt)
@@ -67,11 +74,22 @@ def tile_rulee_kernel(tc, table, w, b, offs, out):
             nc.vector.reciprocal(inv_norm[:], norm[:])
             tn = work.tile([P, CHUNK, D], BF16, name="tn")
             for t in range(CHUNK):
-                nc.vector.tensor_scalar_mul(tn[:, t, :], x[:, t, :], inv_norm[:, t : t + 1])
+                nc.vector.tensor_scalar_mul(tn[:, t, :], x_chunks[c][:, t, :], inv_norm[:, t : t + 1])
+            tn_chunks[c] = tn
+
+        def flip_chunk(c):
             flipped = flip.tile([D, CHUNK * P], BF16, name="flipped")
             for t in range(CHUNK):
-                nc.tensor.transpose(flipped[:, t * P : (t + 1) * P], tn[:, t, :], ident[:])
-            nc.scalar.copy(tnT[:, c * CHUNK * P : (c + 1) * CHUNK * P], flipped[:])
+                nc.tensor.transpose(flipped[:, t * P : (t + 1) * P], tn_chunks[c][:, t, :], ident[:])
+            nc.vector.tensor_copy(tnT[:, c * CHUNK * P : (c + 1) * CHUNK * P], flipped[:])
+
+        for c in range(CHUNKS + 2):
+            if c < CHUNKS:
+                sum_squares(c)
+            if 1 <= c <= CHUNKS:
+                scale(c - 1)
+            if c >= 2:
+                flip_chunk(c - 2)
 
         k = PIECE // 16
         for j in range(PIECES):

@@ -39,10 +39,6 @@ def tile_rulee_kernel(tc, table, w, b, offs, out):
         w_sb = held.tile([D, M], BF16, name="w_sb")
         nc.scalar.dma_start(w_sb[:], w)
 
-        one = held.tile([P, 1], F32, name="one")
-        nc.vector.memset(one[:], 1.0)
-        nc.scalar.activation(one[:], one[:], ACT.Sqrt)
-
         ident_f32 = held.tile([P, P], F32, name="ident_f32")
         make_identity(nc, ident_f32[:])
         ident = held.tile([P, P], BF16, name="ident")
@@ -56,7 +52,9 @@ def tile_rulee_kernel(tc, table, w, b, offs, out):
         nc.vector.tensor_copy(bias[:], b_cols[:, 0:MB])
 
         tnT = held.tile([D, S], BF16, name="tnT")
-        sumsq_chunks, tn_chunks = {}, {}
+        neg_half = held.tile([P, CHUNK], F32, name="neg_half")
+        nc.gpsimd.memset(neg_half[:], -0.5)
+        sumsq_chunks, tn_chunks, flipped_chunks = {}, {}, {}
 
         def sum_squares(c):
             sumsq = work.tile([P, CHUNK], F32, name="sumsq")
@@ -66,12 +64,10 @@ def tile_rulee_kernel(tc, table, w, b, offs, out):
             sumsq_chunks[c] = sumsq
 
         def scale(c):
-            sumsq = sumsq_chunks[c]
-            nc.vector.tensor_scalar_max(sumsq[:], sumsq[:], EPS * EPS)
-            norm = work.tile([P, CHUNK], F32, name="norm")
-            nc.scalar.activation(norm[:], sumsq[:], ACT.Sqrt)
+            clamped = work.tile([P, CHUNK], F32, name="clamped")
+            nc.gpsimd.tensor_scalar_max(clamped[:], sumsq_chunks[c][:], EPS * EPS)
             inv_norm = work.tile([P, CHUNK], F32, name="inv_norm")
-            nc.vector.reciprocal(inv_norm[:], norm[:])
+            nc.gpsimd.tensor_tensor(inv_norm[:], clamped[:], neg_half[:], mybir.AluOpType.pow)
             tn = work.tile([P, CHUNK, D], BF16, name="tn")
             for t in range(CHUNK):
                 nc.vector.tensor_scalar_mul(tn[:, t, :], x_chunks[c][:, t, :], inv_norm[:, t : t + 1])
@@ -81,15 +77,18 @@ def tile_rulee_kernel(tc, table, w, b, offs, out):
             flipped = flip.tile([D, CHUNK * P], BF16, name="flipped")
             for t in range(CHUNK):
                 nc.tensor.transpose(flipped[:, t * P : (t + 1) * P], tn_chunks[c][:, t, :], ident[:])
-            nc.vector.tensor_copy(tnT[:, c * CHUNK * P : (c + 1) * CHUNK * P], flipped[:])
+            flipped_chunks[c] = flipped
 
-        for c in range(CHUNKS + 2):
+        def copy_out(c):
+            nc.vector.tensor_copy(tnT[:, c * CHUNK * P : (c + 1) * CHUNK * P], flipped_chunks[c][:])
+
+        for c in range(CHUNKS + 1):
             if c < CHUNKS:
                 sum_squares(c)
-            if 1 <= c <= CHUNKS:
-                scale(c - 1)
-            if c >= 2:
-                flip_chunk(c - 2)
+                scale(c)
+                flip_chunk(c)
+            if c >= 1:
+                copy_out(c - 1)
 
         k = PIECE // 16
         for j in range(PIECES):

@@ -4,9 +4,11 @@ from concourse.masks import make_identity
 P = 128
 S, D, M, N = 4096, 128, 512, 2048
 EPS = 1e-12
+TINY = 2.0**-112
 
 CHUNK = 4
 CHUNKS = S // (CHUNK * P)
+LAG = 2
 PIECE = 512
 PIECES = N // PIECE
 MB = M // P
@@ -23,7 +25,7 @@ def tile_rulee_kernel(tc, table, w, b, offs, out):
         tc.tile_pool(name="held", bufs=1) as held,
         tc.tile_pool(name="rows", bufs=CHUNKS) as rows,
         tc.tile_pool(name="work", bufs=3) as work,
-        tc.tile_pool(name="staged", bufs=6) as staged,
+        tc.tile_pool(name="staged", bufs=PIECES * MB) as staged,
         tc.psum_pool(name="flip", bufs=3) as flip,
         tc.psum_pool(name="bias_flip", bufs=1) as bias_flip,
         tc.psum_pool(name="products", bufs=4) as products,
@@ -39,6 +41,11 @@ def tile_rulee_kernel(tc, table, w, b, offs, out):
         w_sb = held.tile([D, M], BF16, name="w_sb")
         nc.scalar.dma_start(w_sb[:], w)
 
+        tiny = held.tile([P, 1], F32, name="tiny")
+        nc.vector.memset(tiny[:], TINY)
+        warm = held.tile([P, 1], F32, name="warm")
+        nc.scalar.activation(warm[:], tiny[:], ACT.Sqrt)
+
         ident_f32 = held.tile([P, P], F32, name="ident_f32")
         make_identity(nc, ident_f32[:])
         ident = held.tile([P, P], BF16, name="ident")
@@ -52,22 +59,21 @@ def tile_rulee_kernel(tc, table, w, b, offs, out):
         nc.vector.tensor_copy(bias[:], b_cols[:, 0:MB])
 
         tnT = held.tile([D, S], BF16, name="tnT")
-        neg_half = held.tile([P, CHUNK], F32, name="neg_half")
-        nc.gpsimd.memset(neg_half[:], -0.5)
-        sumsq_chunks, tn_chunks, flipped_chunks = {}, {}, {}
+        norm_chunks, tn_chunks, flipped_chunks = {}, {}, {}
 
-        def sum_squares(c):
+        def norms(c):
             sumsq = work.tile([P, CHUNK], F32, name="sumsq")
             for t in range(CHUNK):
                 squares = work.tile([P, D], BF16, name="squares")
                 nc.scalar.activation(squares[:], x_chunks[c][:, t, :], ACT.Square, accum_out=sumsq[:, t : t + 1])
-            sumsq_chunks[c] = sumsq
+            norm = work.tile([P, CHUNK], F32, name="norm")
+            nc.scalar.activation(norm[:], sumsq[:], ACT.Sqrt, bias=tiny[:])
+            norm_chunks[c] = norm
 
         def scale(c):
-            clamped = work.tile([P, CHUNK], F32, name="clamped")
-            nc.gpsimd.tensor_scalar_max(clamped[:], sumsq_chunks[c][:], EPS * EPS)
             inv_norm = work.tile([P, CHUNK], F32, name="inv_norm")
-            nc.gpsimd.tensor_tensor(inv_norm[:], clamped[:], neg_half[:], mybir.AluOpType.pow)
+            nc.vector.tensor_scalar_max(inv_norm[:], norm_chunks[c][:], EPS)
+            nc.vector.reciprocal(inv_norm[:], inv_norm[:])
             tn = work.tile([P, CHUNK, D], BF16, name="tn")
             for t in range(CHUNK):
                 nc.vector.tensor_scalar_mul(tn[:, t, :], x_chunks[c][:, t, :], inv_norm[:, t : t + 1])
@@ -82,13 +88,13 @@ def tile_rulee_kernel(tc, table, w, b, offs, out):
         def copy_out(c):
             nc.vector.tensor_copy(tnT[:, c * CHUNK * P : (c + 1) * CHUNK * P], flipped_chunks[c][:])
 
-        for c in range(CHUNKS + 1):
+        for c in range(CHUNKS + LAG):
             if c < CHUNKS:
-                sum_squares(c)
+                norms(c)
                 scale(c)
                 flip_chunk(c)
-            if c >= 1:
-                copy_out(c - 1)
+            if c >= LAG:
+                copy_out(c - LAG)
 
         k = PIECE // 16
         for j in range(PIECES):

@@ -82,7 +82,7 @@ def tile_rulee_kernel(tc, table, w, b, offs, out):
         def flip_chunk(c):
             flipped = flip.tile([D, CHUNK * P], BF16, name="flipped")
             for t in range(CHUNK):
-                nc.tensor.transpose(flipped[:, t * P : (t + 1) * P], tn_chunks[c][:, t, :], ident[:])
+                nc.tensor.matmul(flipped[:, t * P : (t + 1) * P], tn_chunks[c][:, t, :], ident[:], start=True, stop=True)
             flipped_chunks[c] = flipped
 
         def copy_out(c):

@@ -9,6 +9,7 @@ TINY = 2.0**-112
 CHUNK = 4
 CHUNKS = S // (CHUNK * P)
 LAG = 2
+EARLY = 3
 PIECE = 512
 PIECES = N // PIECE
 MB = M // P
@@ -17,6 +18,7 @@ FLOPS = 2 * D * M * N
 
 BF16, F32, U16 = mybir.dt.bfloat16, mybir.dt.float32, mybir.dt.uint16
 ACT = mybir.ActivationFunctionType
+MULT = mybir.AluOpType.mult
 
 
 def tile_rulee_kernel(tc, table, w, b, offs, out):
@@ -59,15 +61,28 @@ def tile_rulee_kernel(tc, table, w, b, offs, out):
         nc.vector.tensor_copy(bias[:], b_cols[:, 0:MB])
 
         tnT = held.tile([D, S], BF16, name="tnT")
-        norm_chunks, tn_chunks, flipped_chunks = {}, {}, {}
+        sumsq_chunks, norm_chunks, tn_chunks, flipped_chunks = {}, {}, {}, {}
 
-        def norms(c):
+        def sums_on_scalar(c):
             sumsq = work.tile([P, CHUNK], F32, name="sumsq")
             for t in range(CHUNK):
                 squares = work.tile([P, D], BF16, name="squares")
                 nc.scalar.activation(squares[:], x_chunks[c][:, t, :], ACT.Square, accum_out=sumsq[:, t : t + 1])
+            sumsq_chunks[c] = sumsq
+
+        def sums_on_vector(c):
+            sumsq = held.tile([P, CHUNK], F32, name="sumsq_v")
+            for t in range(CHUNK):
+                x_block = x_chunks[c][:, t, :]
+                squares = work.tile([P, D], BF16, name="squares_v")
+                nc.vector.scalar_tensor_tensor(
+                    squares[:], x_block, 1.0, x_block, op0=MULT, op1=MULT, accum_out=sumsq[:, t : t + 1]
+                )
+            sumsq_chunks[c] = sumsq
+
+        def roots(c):
             norm = work.tile([P, CHUNK], F32, name="norm")
-            nc.scalar.activation(norm[:], sumsq[:], ACT.Sqrt, bias=tiny[:])
+            nc.scalar.activation(norm[:], sumsq_chunks[c][:], ACT.Sqrt, bias=tiny[:])
             norm_chunks[c] = norm
 
         def scale(c):
@@ -89,12 +104,16 @@ def tile_rulee_kernel(tc, table, w, b, offs, out):
             nc.vector.tensor_copy(tnT[:, c * CHUNK * P : (c + 1) * CHUNK * P], flipped_chunks[c][:])
 
         for c in range(CHUNKS + LAG):
+            if c < CHUNKS - 1:
+                sums_on_scalar(c)
             if c < CHUNKS:
-                norms(c)
+                roots(c)
                 scale(c)
                 flip_chunk(c)
             if c >= LAG:
                 copy_out(c - LAG)
+            if c == CHUNKS - 1 - EARLY:
+                sums_on_vector(CHUNKS - 1)
 
         k = PIECE // 16
         for j in range(PIECES):

@@ -8,8 +8,8 @@ TINY = 2.0**-112
 
 CHUNK = 4
 CHUNKS = S // (CHUNK * P)
+WARM = 8
 LAG = 2
-EARLY = 3
 PIECE = 512
 PIECES = N // PIECE
 MB = M // P
@@ -18,7 +18,6 @@ FLOPS = 2 * D * M * N
 
 BF16, F32, U16 = mybir.dt.bfloat16, mybir.dt.float32, mybir.dt.uint16
 ACT = mybir.ActivationFunctionType
-MULT = mybir.AluOpType.mult
 
 
 def tile_rulee_kernel(tc, table, w, b, offs, out):
@@ -29,7 +28,7 @@ def tile_rulee_kernel(tc, table, w, b, offs, out):
         tc.tile_pool(name="work", bufs=3) as work,
         tc.tile_pool(name="staged", bufs=PIECES * MB) as staged,
         tc.psum_pool(name="flip", bufs=3) as flip,
-        tc.psum_pool(name="bias_flip", bufs=1) as bias_flip,
+        tc.psum_pool(name="spare", bufs=1) as spare,
         tc.psum_pool(name="products", bufs=4) as products,
     ):
         table_blocks = table.rearrange("(t p) d -> p t d", p=P)
@@ -48,6 +47,12 @@ def tile_rulee_kernel(tc, table, w, b, offs, out):
         warm = held.tile([P, 1], F32, name="warm")
         nc.scalar.activation(warm[:], tiny[:], ACT.Sqrt)
 
+        zeros = held.tile([P, PIECE], BF16, name="zeros")
+        nc.vector.memset(zeros[:], 0.0)
+        unread = spare.tile([P, PIECE], F32, name="unread", tag="spare")
+        for warm_up in range(WARM):
+            nc.tensor.matmul(unread[:], zeros[:, 0:P], zeros[:], start=True, stop=True)
+
         ident_f32 = held.tile([P, P], F32, name="ident_f32")
         make_identity(nc, ident_f32[:])
         ident = held.tile([P, P], BF16, name="ident")
@@ -55,34 +60,21 @@ def tile_rulee_kernel(tc, table, w, b, offs, out):
         b_rows = held.tile([P, P], F32, name="b_rows")
         nc.vector.memset(b_rows[:], 0.0)
         nc.scalar.dma_start(b_rows[0:MB, :], b.rearrange("(mb p) one -> mb (p one)", p=P))
-        b_cols = bias_flip.tile([P, P], F32, name="b_cols")
+        b_cols = spare.tile([P, P], F32, name="b_cols", tag="spare")
         nc.tensor.transpose(b_cols[:], b_rows[:], ident_f32[:])
         bias = held.tile([P, MB], F32, name="bias")
         nc.vector.tensor_copy(bias[:], b_cols[:, 0:MB])
 
         tnT = held.tile([D, S], BF16, name="tnT")
-        sumsq_chunks, norm_chunks, tn_chunks, flipped_chunks = {}, {}, {}, {}
+        norm_chunks, tn_chunks, flipped_chunks = {}, {}, {}
 
-        def sums_on_scalar(c):
+        def norms(c):
             sumsq = work.tile([P, CHUNK], F32, name="sumsq")
             for t in range(CHUNK):
                 squares = work.tile([P, D], BF16, name="squares")
                 nc.scalar.activation(squares[:], x_chunks[c][:, t, :], ACT.Square, accum_out=sumsq[:, t : t + 1])
-            sumsq_chunks[c] = sumsq
-
-        def sums_on_vector(c):
-            sumsq = held.tile([P, CHUNK], F32, name="sumsq_v")
-            for t in range(CHUNK):
-                x_block = x_chunks[c][:, t, :]
-                squares = work.tile([P, D], BF16, name="squares_v")
-                nc.vector.scalar_tensor_tensor(
-                    squares[:], x_block, 1.0, x_block, op0=MULT, op1=MULT, accum_out=sumsq[:, t : t + 1]
-                )
-            sumsq_chunks[c] = sumsq
-
-        def roots(c):
             norm = work.tile([P, CHUNK], F32, name="norm")
-            nc.scalar.activation(norm[:], sumsq_chunks[c][:], ACT.Sqrt, bias=tiny[:])
+            nc.scalar.activation(norm[:], sumsq[:], ACT.Sqrt, bias=tiny[:])
             norm_chunks[c] = norm
 
         def scale(c):
@@ -104,16 +96,12 @@ def tile_rulee_kernel(tc, table, w, b, offs, out):
             nc.vector.tensor_copy(tnT[:, c * CHUNK * P : (c + 1) * CHUNK * P], flipped_chunks[c][:])
 
         for c in range(CHUNKS + LAG):
-            if c < CHUNKS - 1:
-                sums_on_scalar(c)
             if c < CHUNKS:
-                roots(c)
+                norms(c)
                 scale(c)
                 flip_chunk(c)
             if c >= LAG:
                 copy_out(c - LAG)
-            if c == CHUNKS - 1 - EARLY:
-                sums_on_vector(CHUNKS - 1)
 
         k = PIECE // 16
         for j in range(PIECES):

@@ -4,7 +4,7 @@ from concourse.masks import make_identity
 P = 128
 S, D, M, N = 4096, 128, 512, 2048
 EPS = 1e-12
-TINY = 2.0**-112
+FLOOR = EPS * EPS
 
 CHUNK = 4
 CHUNKS = S // (CHUNK * P)
@@ -18,6 +18,7 @@ FLOPS = 2 * D * M * N
 
 BF16, F32, U16 = mybir.dt.bfloat16, mybir.dt.float32, mybir.dt.uint16
 ACT = mybir.ActivationFunctionType
+ALU = mybir.AluOpType
 
 
 def tile_rulee_kernel(tc, table, w, b, offs, out):
@@ -42,10 +43,12 @@ def tile_rulee_kernel(tc, table, w, b, offs, out):
         w_sb = held.tile([D, M], BF16, name="w_sb")
         nc.scalar.dma_start(w_sb[:], w)
 
-        tiny = held.tile([P, 1], F32, name="tiny")
-        nc.vector.memset(tiny[:], TINY)
+        floor = held.tile([P, 1], F32, name="floor")
+        nc.vector.memset(floor[:], FLOOR)
+        minus_floor = held.tile([P, 1], F32, name="minus_floor")
+        nc.vector.memset(minus_floor[:], -FLOOR)
         warm = held.tile([P, 1], F32, name="warm")
-        nc.scalar.activation(warm[:], tiny[:], ACT.Sqrt)
+        nc.scalar.activation(warm[:], floor[:], ACT.Abs_reciprocal_sqrt)
 
         zeros = held.tile([P, PIECE], BF16, name="zeros")
         nc.vector.memset(zeros[:], 0.0)
@@ -71,19 +74,25 @@ def tile_rulee_kernel(tc, table, w, b, offs, out):
         def norms(c):
             sumsq = work.tile([P, CHUNK], F32, name="sumsq")
             for t in range(CHUNK):
-                squares = work.tile([P, D], BF16, name="squares")
-                nc.scalar.activation(squares[:], x_chunks[c][:, t, :], ACT.Square, accum_out=sumsq[:, t : t + 1])
-            norm = work.tile([P, CHUNK], F32, name="norm")
-            nc.scalar.activation(norm[:], sumsq[:], ACT.Sqrt, bias=tiny[:])
-            norm_chunks[c] = norm
+                block = x_chunks[c][:, t, :]
+                if t < CHUNK - 1:
+                    squares = work.tile([P, D], BF16, name="squares")
+                    nc.scalar.activation(squares[:], block, ACT.Square, accum_out=sumsq[:, t : t + 1])
+                else:
+                    squares_v = work.tile([P, D], F32, name="squares_v")
+                    nc.vector.scalar_tensor_tensor(
+                        squares_v[:], block, 1.0, block, op0=ALU.mult, op1=ALU.mult, accum_out=sumsq[:, t : t + 1]
+                    )
+            excess = work.tile([P, CHUNK], F32, name="excess")
+            nc.scalar.activation(excess[:], sumsq[:], ACT.Relu, bias=minus_floor[:])
+            inv_norm = work.tile([P, CHUNK], F32, name="inv_norm")
+            nc.scalar.activation(inv_norm[:], excess[:], ACT.Abs_reciprocal_sqrt, bias=floor[:])
+            norm_chunks[c] = inv_norm
 
         def scale(c):
-            inv_norm = work.tile([P, CHUNK], F32, name="inv_norm")
-            nc.vector.tensor_scalar_max(inv_norm[:], norm_chunks[c][:], EPS)
-            nc.vector.reciprocal(inv_norm[:], inv_norm[:])
             tn = work.tile([P, CHUNK, D], BF16, name="tn")
             for t in range(CHUNK):
-                nc.vector.tensor_scalar_mul(tn[:, t, :], x_chunks[c][:, t, :], inv_norm[:, t : t + 1])
+                nc.vector.tensor_scalar_mul(tn[:, t, :], x_chunks[c][:, t, :], norm_chunks[c][:, t : t + 1])
             tn_chunks[c] = tn
 
         def flip_chunk(c):

@@ -41,7 +41,7 @@ def tile_rulee_kernel(tc, table, w, b, offs, out):
         offsets = held.tile([P, N // 16], U16, name="offsets")
         nc.sync.dma_start(offsets[:], offs)
         w_sb = held.tile([D, M], BF16, name="w_sb")
-        nc.scalar.dma_start(w_sb[:], w)
+        nc.sync.dma_start(w_sb[:], w)
 
         floor = held.tile([P, 1], F32, name="floor")
         nc.vector.memset(floor[:], FLOOR)

@@ -8,7 +8,6 @@ FLOOR = EPS * EPS
 
 CHUNK = 4
 CHUNKS = S // (CHUNK * P)
-WARM = 8
 LAG = 2
 PIECE = 512
 PIECES = N // PIECE
@@ -49,12 +48,6 @@ def tile_rulee_kernel(tc, table, w, b, offs, out):
         nc.vector.memset(minus_floor[:], -FLOOR)
         warm = held.tile([P, 1], F32, name="warm")
         nc.scalar.activation(warm[:], floor[:], ACT.Abs_reciprocal_sqrt)
-
-        zeros = held.tile([P, PIECE], BF16, name="zeros")
-        nc.vector.memset(zeros[:], 0.0)
-        unread = spare.tile([P, PIECE], F32, name="unread", tag="spare")
-        for warm_up in range(WARM):
-            nc.tensor.matmul(unread[:], zeros[:, 0:P], zeros[:], start=True, stop=True)
 
         ident_f32 = held.tile([P, P], F32, name="ident_f32")
         make_identity(nc, ident_f32[:])

@@ -24,7 +24,7 @@ def tile_rulee_kernel(tc, table, w, b, offs, out):
     nc = tc.nc
     with (
         tc.tile_pool(name="held", bufs=1) as held,
-        tc.tile_pool(name="rows", bufs=CHUNKS) as rows,
+        tc.tile_pool(name="rows", bufs=CHUNKS - 1 + CHUNK) as rows,
         tc.tile_pool(name="work", bufs=3) as work,
         tc.tile_pool(name="staged", bufs=PIECES * MB) as staged,
         tc.psum_pool(name="flip", bufs=3) as flip,
@@ -32,11 +32,13 @@ def tile_rulee_kernel(tc, table, w, b, offs, out):
         tc.psum_pool(name="products", bufs=4) as products,
     ):
         table_blocks = table.rearrange("(t p) d -> p t d", p=P)
-        x_chunks = []
-        for c in range(CHUNKS):
-            x = rows.tile([P, CHUNK, D], BF16, name="x")
-            nc.sync.dma_start(x[:], table_blocks[:, c * CHUNK : (c + 1) * CHUNK, :])
-            x_chunks.append(x)
+        x_blocks = []
+        last = (CHUNKS - 1) * CHUNK
+        for first, blocks in [(c * CHUNK, CHUNK) for c in range(CHUNKS - 1)] + [(last + t, 1) for t in range(CHUNK)]:
+            x = rows.tile([P, blocks, D], BF16, name="x")
+            nc.sync.dma_start(x[:], table_blocks[:, first : first + blocks, :])
+            for t in range(blocks):
+                x_blocks.append(x[:, t, :])
         offsets = held.tile([P, N // 16], U16, name="offsets")
         nc.sync.dma_start(offsets[:], offs)
         w_sb = held.tile([D, M], BF16, name="w_sb")
@@ -67,7 +69,7 @@ def tile_rulee_kernel(tc, table, w, b, offs, out):
         def norms(c):
             sumsq = work.tile([P, CHUNK], F32, name="sumsq")
             for t in range(CHUNK):
-                block = x_chunks[c][:, t, :]
+                block = x_blocks[c * CHUNK + t]
                 if t < CHUNK - 1:
                     squares = work.tile([P, D], BF16, name="squares")
                     nc.scalar.activation(squares[:], block, ACT.Square, accum_out=sumsq[:, t : t + 1])
@@ -85,7 +87,7 @@ def tile_rulee_kernel(tc, table, w, b, offs, out):
         def scale(c):
             tn = work.tile([P, CHUNK, D], BF16, name="tn")
             for t in range(CHUNK):
-                nc.vector.tensor_scalar_mul(tn[:, t, :], x_chunks[c][:, t, :], norm_chunks[c][:, t : t + 1])
+                nc.vector.tensor_scalar_mul(tn[:, t, :], x_blocks[c * CHUNK + t], norm_chunks[c][:, t : t + 1])
             tn_chunks[c] = tn
 
         def flip_chunk(c):

@@ -27,8 +27,7 @@ def tile_rulee_kernel(tc, table, w, b, offs, out):
         tc.tile_pool(name="rows", bufs=CHUNKS - 1 + CHUNK) as rows,
         tc.tile_pool(name="work", bufs=3) as work,
         tc.tile_pool(name="staged", bufs=PIECES * MB) as staged,
-        tc.psum_pool(name="flip", bufs=3) as flip,
-        tc.psum_pool(name="spare", bufs=1) as spare,
+        tc.psum_pool(name="flip", bufs=4) as flip,
         tc.psum_pool(name="products", bufs=4) as products,
     ):
         table_blocks = table.rearrange("(t p) d -> p t d", p=P)
@@ -58,13 +57,13 @@ def tile_rulee_kernel(tc, table, w, b, offs, out):
         b_rows = held.tile([P, P], F32, name="b_rows")
         nc.vector.memset(b_rows[:], 0.0)
         nc.scalar.dma_start(b_rows[0:MB, :], b.rearrange("(mb p) one -> mb (p one)", p=P))
-        b_cols = spare.tile([P, P], F32, name="b_cols", tag="spare")
+        b_cols = flip.tile([P, P], F32, name="b_cols", tag="flipped")
         nc.tensor.transpose(b_cols[:], b_rows[:], ident_f32[:])
         bias = held.tile([P, MB], F32, name="bias")
         nc.vector.tensor_copy(bias[:], b_cols[:, 0:MB])
 
         tnT = held.tile([D, S], BF16, name="tnT")
-        norm_chunks, tn_chunks, flipped_chunks = {}, {}, {}
+        norm_chunks, tn_chunks, flipped_banks = {}, {}, {}
 
         def norms(c):
             sumsq = work.tile([P, CHUNK], F32, name="sumsq")
@@ -91,13 +90,19 @@ def tile_rulee_kernel(tc, table, w, b, offs, out):
             tn_chunks[c] = tn
 
         def flip_chunk(c):
-            flipped = flip.tile([D, CHUNK * P], BF16, name="flipped")
-            for t in range(CHUNK):
-                nc.tensor.matmul(flipped[:, t * P : (t + 1) * P], tn_chunks[c][:, t, :], ident[:], start=True, stop=True)
-            flipped_chunks[c] = flipped
+            blocks = CHUNK if c < CHUNKS - 1 else CHUNK // 2
+            for first in range(0, CHUNK, blocks):
+                flipped = flip.tile([D, blocks * P], BF16, name="flipped")
+                for t in range(blocks):
+                    scaled = tn_chunks[c][:, first + t, :]
+                    nc.tensor.matmul(flipped[:, t * P : (t + 1) * P], scaled, ident[:], start=True, stop=True)
+                flipped_banks[c, first] = flipped
 
         def copy_out(c):
-            nc.vector.tensor_copy(tnT[:, c * CHUNK * P : (c + 1) * CHUNK * P], flipped_chunks[c][:])
+            for first in range(0, CHUNK, CHUNK if c < CHUNKS - 1 else CHUNK // 2):
+                bank = flipped_banks[c, first]
+                a = (c * CHUNK + first) * P
+                nc.vector.tensor_copy(tnT[:, a : a + bank.shape[1]], bank[:])
 
         for c in range(CHUNKS + LAG):
             if c < CHUNKS:

import concourse.mybir as mybir
from concourse.masks import make_identity

P = 128
S, D, M, N = 4096, 128, 512, 2048
EPS = 1e-12
FLOOR = EPS * EPS

CHUNK = 4
CHUNKS = S // (CHUNK * P)
LAG = 2
PIECE = 512
PIECES = N // PIECE
MB = M // P

FLOPS = 2 * D * M * N

BF16, F32, U16 = mybir.dt.bfloat16, mybir.dt.float32, mybir.dt.uint16
ACT = mybir.ActivationFunctionType
ALU = mybir.AluOpType


def tile_rulee_kernel(tc, table, w, b, offs, out):
    nc = tc.nc
    with (
        tc.tile_pool(name="held", bufs=1) as held,
        tc.tile_pool(name="rows", bufs=CHUNKS - 1 + CHUNK) as rows,
        tc.tile_pool(name="work", bufs=3) as work,
        tc.tile_pool(name="staged", bufs=PIECES * MB) as staged,
        tc.psum_pool(name="flip", bufs=4) as flip,
        tc.psum_pool(name="products", bufs=4) as products,
    ):
        table_blocks = table.rearrange("(t p) d -> p t d", p=P)
        x_blocks = []
        last = (CHUNKS - 1) * CHUNK
        for first, blocks in [(c * CHUNK, CHUNK) for c in range(CHUNKS - 1)] + [(last + t, 1) for t in range(CHUNK)]:
            x = rows.tile([P, blocks, D], BF16, name="x")
            nc.sync.dma_start(x[:], table_blocks[:, first : first + blocks, :])
            for t in range(blocks):
                x_blocks.append(x[:, t, :])
        offsets = held.tile([P, N // 16], U16, name="offsets")
        nc.sync.dma_start(offsets[:], offs)
        w_sb = held.tile([D, M], BF16, name="w_sb")
        nc.sync.dma_start(w_sb[:], w)

        floor = held.tile([P, 1], F32, name="floor")
        nc.vector.memset(floor[:], FLOOR)
        minus_floor = held.tile([P, 1], F32, name="minus_floor")
        nc.vector.memset(minus_floor[:], -FLOOR)
        warm = held.tile([P, 1], F32, name="warm")
        nc.scalar.activation(warm[:], floor[:], ACT.Abs_reciprocal_sqrt)

        ident_f32 = held.tile([P, P], F32, name="ident_f32")
        make_identity(nc, ident_f32[:])
        ident = held.tile([P, P], BF16, name="ident")
        make_identity(nc, ident[:])
        b_rows = held.tile([P, P], F32, name="b_rows")
        nc.vector.memset(b_rows[:], 0.0)
        nc.scalar.dma_start(b_rows[0:MB, :], b.rearrange("(mb p) one -> mb (p one)", p=P))
        b_cols = flip.tile([P, P], F32, name="b_cols", tag="flipped")
        nc.tensor.transpose(b_cols[:], b_rows[:], ident_f32[:])
        bias = held.tile([P, MB], F32, name="bias")
        nc.vector.tensor_copy(bias[:], b_cols[:, 0:MB])

        tnT = held.tile([D, S], BF16, name="tnT")
        norm_chunks, tn_chunks, flipped_banks = {}, {}, {}

        def norms(c):
            sumsq = work.tile([P, CHUNK], F32, name="sumsq")
            for t in range(CHUNK):
                block = x_blocks[c * CHUNK + t]
                if t < CHUNK - 1:
                    squares = work.tile([P, D], BF16, name="squares")
                    nc.scalar.activation(squares[:], block, ACT.Square, accum_out=sumsq[:, t : t + 1])
                else:
                    squares_v = work.tile([P, D], F32, name="squares_v")
                    nc.vector.scalar_tensor_tensor(
                        squares_v[:], block, 1.0, block, op0=ALU.mult, op1=ALU.mult, accum_out=sumsq[:, t : t + 1]
                    )
            excess = work.tile([P, CHUNK], F32, name="excess")
            nc.scalar.activation(excess[:], sumsq[:], ACT.Relu, bias=minus_floor[:])
            inv_norm = work.tile([P, CHUNK], F32, name="inv_norm")
            nc.scalar.activation(inv_norm[:], excess[:], ACT.Abs_reciprocal_sqrt, bias=floor[:])
            norm_chunks[c] = inv_norm

        def scale(c):
            tn = work.tile([P, CHUNK, D], BF16, name="tn")
            for t in range(CHUNK):
                nc.vector.tensor_scalar_mul(tn[:, t, :], x_blocks[c * CHUNK + t], norm_chunks[c][:, t : t + 1])
            tn_chunks[c] = tn

        def flip_chunk(c):
            blocks = CHUNK if c < CHUNKS - 1 else CHUNK // 2
            for first in range(0, CHUNK, blocks):
                flipped = flip.tile([D, blocks * P], BF16, name="flipped")
                for t in range(blocks):
                    scaled = tn_chunks[c][:, first + t, :]
                    nc.tensor.matmul(flipped[:, t * P : (t + 1) * P], scaled, ident[:], start=True, stop=True)
                flipped_banks[c, first] = flipped

        def copy_out(c):
            for first in range(0, CHUNK, CHUNK if c < CHUNKS - 1 else CHUNK // 2):
                bank = flipped_banks[c, first]
                a = (c * CHUNK + first) * P
                nc.vector.tensor_copy(tnT[:, a : a + bank.shape[1]], bank[:])

        for c in range(CHUNKS + LAG):
            if c < CHUNKS:
                norms(c)
                scale(c)
                flip_chunk(c)
            if c >= LAG:
                copy_out(c - LAG)

        k = PIECE // 16
        for j in range(PIECES):
            for mb in range(MB):
                product = products.tile([P, PIECE], F32, name="product")
                nc.tensor.matmul(
                    product[:],
                    w_sb[:, mb * P : (mb + 1) * P],
                    tnT[:].indirect(offsets[:, j * k : (j + 1) * k]),
                    start=True,
                    stop=True,
                )
                result = staged.tile([P, PIECE], F32, name="result")
                if mb % 2 == 0:
                    nc.vector.tensor_scalar_add(result[:], product[:], bias[:, mb : mb + 1])
                else:
                    nc.scalar.activation(result[:], product[:], ACT.Identity, bias=bias[:, mb : mb + 1])
                nc.sync.dma_start(out[mb * P : (mb + 1) * P, j * PIECE : (j + 1) * PIECE], result[:])
